import numpy as np
import ml_dtypes


def mxq(x, axis, fmt="e4m3"):
    dtype, down = {"e4m3": (ml_dtypes.float8_e4m3fn, 7), "e5m2": (ml_dtypes.float8_e5m2, 14)}[fmt]
    v = np.moveaxis(np.asarray(x, np.float32).astype(ml_dtypes.bfloat16).astype(np.float64), axis, -1)
    blocks = v.reshape(v.shape[:-1] + (-1, 32))
    amax = np.abs(blocks).max(-1, keepdims=True)
    byte = np.maximum(np.where(amax > 0, np.frexp(amax)[1] - 1 + 127, 0) - down, 1)
    scale = np.exp2(byte - 127.0)
    codes = (blocks / scale).astype(np.float32).astype(dtype).astype(np.float64)
    return np.moveaxis((codes * scale).reshape(v.shape), -1, axis)


WIDE = False


def mx_kscale(k):
    if not WIDE:
        return np.ones(k)
    levels = np.array([10, -10, 5, -5, 0])
    a = np.random.permutation(np.resize(levels, k // 512 * 4)).reshape(k // 512, 4)
    idx = np.arange(k)
    return np.exp2(a[idx // 512, idx % 128 // 32])


BF16 = ml_dtypes.bfloat16


def bf(x):
    return np.asarray(x, np.float32).astype(BF16)


def f64(x):
    return np.asarray(x).astype(np.float64)


B, D, F, P = 8192, 512, 512, 128
GAIN = 4.0 / np.sqrt(F)


def sigmoid(v):
    return 1.0 / (1.0 + np.exp(-v))


def setup_inputs():
    s = mx_kscale(D)
    return {
        "x": bf(np.random.standard_normal((B, D)) * s),
        "features": bf(np.random.standard_normal((F, D)) / np.sqrt(D) / s),
        "prototypes": bf(np.random.standard_normal((P, D)) * s),
        "alpha": bf((0.5 + 0.05 * np.random.standard_normal(1)) * GAIN),
        "beta": bf((0.3 + 0.03 * np.random.standard_normal(1)) * GAIN),
        "theta": bf((2.0 + 0.1 * np.random.standard_normal(1)) * GAIN),
    }


def reference(x, features, prototypes, alpha, beta, theta):
    fq = mxq(f64(features), 1, "e4m3")
    xf = mxq(f64(x), 1, "e4m3") @ fq.T
    pf = mxq(f64(prototypes), 1, "e4m3") @ fq.T
    sx = sigmoid(xf)
    sp = sigmoid(pf)
    ax = xf * sx
    bp = pf * sp
    axq = mxq(ax, 1, "e4m3")
    bpq = mxq(bp, 1, "e4m3")
    sxq = mxq(sx, 1, "e4m3")
    spq = mxq(sp, 1, "e4m3")
    common = axq @ bpq.T
    x_distinctive = ax.sum(axis=1, keepdims=True) - (axq @ spq.T)
    p_distinctive = bp.sum(axis=1)[None, :] - (sxq @ bpq.T)
    return f64(theta) * common - f64(alpha) * x_distinctive - f64(beta) * p_distinctive

@@ -1,0 +1,379 @@
+from contextlib import ExitStack
+
+import concourse.mybir as mybir
+from concourse.masks import make_identity
+
+F32 = mybir.dt.float32
+BF16 = mybir.dt.bfloat16
+U32 = mybir.dt.uint32
+U8 = mybir.dt.uint8
+FP8X4 = mybir.dt.float8_e4m3fn_x4
+ACT = mybir.ActivationFunctionType
+ALU = mybir.AluOpType
+
+P = 128
+B, D, F, NP = 8192, 512, 512, 128
+NCH = B // P
+NG = NCH // 4
+NH = NCH // 2
+FLOPS = 2 * (B + NP) * D * F + 3 * 2 * B * F * NP
+
+ACT_EA_FROM = 1
+ACT_EA_SKIP = 99
+HEAD_ACT_E = 1
+
+
+def tile_tverskylayer_pa_t_kernel(tc, x, features, prototypes, alpha, beta, theta, out):
+    nc = tc.nc
+    with ExitStack() as ctx:
+        ctx.enter_context(tc.manual_schedule())
+        const = ctx.enter_context(tc.tile_pool(name="const", bufs=1))
+        xin_pool = ctx.enter_context(tc.tile_pool(name="xin", bufs=6))
+        grp_pool = ctx.enter_context(tc.tile_pool(name="grp", bufs=3))
+        ax_pool = ctx.enter_context(tc.tile_pool(name="axp", bufs=6))
+        fin_pool = ctx.enter_context(tc.tile_pool(name="fin", bufs=3))
+        psum = ctx.enter_context(tc.psum_pool(name="ps", bufs=1))
+
+        def bank(i, shape, dtype, name):
+            return psum.tile(shape, dtype, name=name, tag="bank%d" % i)
+
+        x_rows = x.rearrange("(p c) d -> p (c d)", c=NCH)
+        out_rows = out.rearrange("(p c) q -> p (c q)", c=NCH)
+
+        ident_f = const.tile([P, P], F32, name="ident_f")
+        make_identity(nc, ident_f[:])
+        ident_b = const.tile([P, P], BF16, name="ident_b")
+        make_identity(nc, ident_b[:])
+        ones_f = const.tile([P, P], F32, name="ones_f")
+        nc.vector.memset(ones_f[:], 1.0)
+        warm = const.tile([P, 1], F32, name="warm")
+        nc.scalar.activation(out=warm[:], in_=ones_f[:, 0:1], func=ACT.Sigmoid)
+
+        f_sb = const.tile([P, 4 * D], BF16, name="f_sb")
+        p_sb = const.tile([P, D], BF16, name="p_sb")
+        a_bf = const.tile([P, 1], BF16, name="a_bf")
+        b_bf = const.tile([P, 1], BF16, name="b_bf")
+        t_bf = const.tile([P, 1], BF16, name="t_bf")
+        gf = const.tile([P, 4 * F], BF16, name="gf", align_bytes=64)
+        gp = const.tile([P, 4 * NP], BF16, name="gp", align_bytes=64)
+        fq = const.tile([P, F], U32, name="fq", align_bytes=64)
+        fs = const.tile([P, F], U8, name="fs", align_bytes=64)
+        pq = const.tile([P, NP], U32, name="pq", align_bytes=64)
+        pscl = const.tile([P, NP], U8, name="pscl", align_bytes=64)
+        xq = const.tile([P, B], U32, name="xq", align_bytes=64)
+        xs = const.tile([P, B], U8, name="xs", align_bytes=64)
+        sxq = const.tile([P, B], U32, name="sxq", align_bytes=64)
+        sxs = const.tile([P, B], U8, name="sxs", align_bytes=64)
+        sp32 = const.tile([P, F], F32, name="sp32")
+        bp32 = const.tile([P, F], F32, name="bp32")
+        gbs = const.tile([P, 8 * NP], BF16, name="gbs", align_bytes=64)
+        bsq = const.tile([P, 2 * NP], U32, name="bsq", align_bytes=64)
+        bss = const.tile([P, 2 * NP], U8, name="bss", align_bytes=64)
+        krow = const.tile([P, NP], F32, name="krow")
+        a32 = const.tile([P, 1], F32, name="a32")
+        b32 = const.tile([P, 1], F32, name="b32")
+        t32 = const.tile([P, 1], F32, name="t32")
+        na32 = const.tile([P, 1], F32, name="na32")
+        nb32 = const.tile([P, 1], F32, name="nb32")
+
+        xin = {}
+
+        def load_x(g, pieces=1):
+            xin[g] = xin_pool.tile([P, 4 * D], BF16, name="xin%d" % g, tag="xin")
+            w = 4 * D // pieces
+            for k in range(pieces):
+                nc.sync.dma_start(
+                    out=xin[g][:, w * k : w * (k + 1)], in_=x_rows[:, 4 * D * g + w * k : 4 * D * g + w * (k + 1)]
+                )
+
+        nc.sync.dma_start(out=f_sb[:], in_=features.rearrange("(p t) d -> p (t d)", t=4))
+        load_x(0, pieces=2)
+        for g in range(1, 6):
+            load_x(g)
+
+        def word_transposes(src_words, first_chunk, n_chunks, pbank):
+            for j in range(n_chunks):
+                for u in range(2):
+                    nc.tensor.transpose(
+                        pbank[:, P * (2 * j + u) : P * (2 * j + u + 1)],
+                        src_words[:, 256 * (first_chunk + j) + P * u : 256 * (first_chunk + j) + P * (u + 1)],
+                        ident_f[:],
+                    )
+
+        def exit_words(copy, dst_words, first_chunk, n_chunks, pbank):
+            copy(
+                out=dst_words[:, 256 * first_chunk : 256 * (first_chunk + n_chunks)].rearrange(
+                    "p (c b u) -> p c b u", c=n_chunks, u=2
+                ),
+                in_=pbank[:, 0 : 256 * n_chunks].rearrange("p (c u b) -> p c b u", c=n_chunks, u=2),
+            )
+
+        def quantise(codes, scales, src):
+            nc.vector.quantize_mx(out=codes.bitcast(FP8X4), scales=scales, in_=src)
+
+        def mx(o, l, ls, r, rs_):
+            nc.tensor.matmul_mx(
+                out=o, lhsT=l.bitcast(FP8X4), lhsT_scale=ls, rhs=r.bitcast(FP8X4), rhs_scale=rs_, start=True, stop=True
+            )
+
+        xt = {}
+        gx = {}
+
+        def t_x(g):
+            xw = xin[g][:].bitcast(F32)
+            for k in range(2):
+                xt[(g, k)] = bank((2 * g + k) % 4, [P, 512], F32, "xt%d_%d" % (g, k))
+                word_transposes(xw, 2 * k, 2, xt[(g, k)])
+
+        def e_x(g, k, copy):
+            if k == 0:
+                gx[g] = grp_pool.tile([P, 2048], BF16, name="gx%d" % g, tag="gx", align_bytes=64)
+            exit_words(copy, gx[g][:].bitcast(F32), 2 * k, 2, xt[(g, k)])
+
+        def q_x(g, first=0, n=4):
+            lo, hi = 512 * g + P * first, 512 * g + P * (first + n)
+            quantise(xq[:, lo:hi], xs[:, lo:hi], gx[g][:, 512 * first : 512 * (first + n)])
+
+        fw = f_sb[:].bitcast(F32)
+        gfw = gf[:].bitcast(F32)
+        ft = [bank(4 + j, [P, 512], F32, "ft%d" % j) for j in range(2)]
+        for j in range(2):
+            word_transposes(fw, 2 * j, 2, ft[j])
+        exit_words(nc.vector.tensor_copy, gfw, 0, 2, ft[0])
+        exit_words(nc.scalar.copy, gfw, 2, 2, ft[1])
+        t_x(0)
+        load_x(6)
+        quantise(fq[:], fs[:], gf[:])
+        e_x(0, 0, nc.scalar.copy if HEAD_ACT_E else nc.vector.tensor_copy)
+        t_x(1)
+        load_x(7)
+        e_x(0, 1, nc.vector.tensor_copy)
+        q_x(0, 0, 2)
+        e_x(1, 0, nc.vector.tensor_copy)
+        q_x(0, 2, 2)
+        e_x(1, 1, nc.vector.tensor_copy)
+        q_x(1)
+
+        gs = {}
+
+        def o1_sig(c):
+            g, c4 = c // 4, c % 4
+            if c4 == 0:
+                gs[g] = grp_pool.tile([P, 2048], BF16, name="gs%d" % g, tag="gs", align_bytes=64)
+            o1 = bank(4 + c4, [P, 512], F32, "o1_%d" % c)
+            for t in range(4):
+                mx(
+                    o1[:, P * t : P * (t + 1)],
+                    fq[:, P * t : P * (t + 1)],
+                    fs[:, P * t : P * (t + 1)],
+                    xq[:, P * c : P * (c + 1)],
+                    xs[:, P * c : P * (c + 1)],
+                )
+            nc.scalar.activation(
+                out=gs[g][:, 512 * c4 : 512 * (c4 + 1)].rearrange("p (b t) -> p b t", t=4),
+                in_=o1[:].rearrange("p (t b) -> p b t", t=4),
+                func=ACT.Sigmoid,
+            )
+
+        def q_s(g):
+            quantise(sxq[:, 512 * g : 512 * (g + 1)], sxs[:, 512 * g : 512 * (g + 1)], gs[g][:])
+
+        for i in range(NG):
+            if i + 2 < NG:
+                t_x(i + 2)
+            if i + 8 < NG:
+                load_x(i + 8)
+            if i == 8:
+                nc.sync.dma_start(out=p_sb[:], in_=prototypes)
+                nc.sync.dma_start(out=a_bf[:], in_=alpha.partition_broadcast(P))
+                nc.sync.dma_start(out=b_bf[:], in_=beta.partition_broadcast(P))
+                nc.sync.dma_start(out=t_bf[:], in_=theta.partition_broadcast(P))
+            if i == NG - 2:
+                pt = bank(0, [P, 512], F32, "pt")
+                word_transposes(p_sb[:].bitcast(F32), 0, 1, pt)
+            for c4 in range(4):
+                o1_sig(4 * i + c4)
+            if i + 2 < NG:
+                e_x(i + 2, 0, nc.vector.tensor_copy)
+                e_x(i + 2, 1, nc.vector.tensor_copy)
+            if i >= 1:
+                q_s(i - 1)
+            if i + 2 < NG:
+                q_x(i + 2)
+            if i == NG - 2:
+                exit_words(nc.vector.tensor_copy, gp[:].bitcast(F32), 0, 1, pt)
+                nc.vector.tensor_copy(out=a32[:], in_=a_bf[:])
+                nc.vector.tensor_copy(out=b32[:], in_=b_bf[:])
+                nc.vector.tensor_copy(out=t32[:], in_=t_bf[:])
+                nc.vector.tensor_scalar_mul(out=na32[:], in0=a32[:], scalar1=-1.0)
+                nc.vector.tensor_scalar_mul(out=nb32[:], in0=b32[:], scalar1=-1.0)
+                quantise(pq[:], pscl[:], gp[:])
+
+        pf = bank(3, [P, 512], F32, "pf")
+        for t in range(4):
+            mx(pf[:, P * t : P * (t + 1)], fq[:, P * t : P * (t + 1)], fs[:, P * t : P * (t + 1)], pq[:], pscl[:])
+        nc.scalar.activation(out=sp32[:], in_=pf[:], func=ACT.Sigmoid)
+
+        o2 = {}
+        axs = {}
+        rs = {}
+        at = {}
+        ga = {}
+        unit = {}
+
+        def o2_pass(c):
+            o2[c] = bank(c % 3, [P, 512], F32, "o2_%d" % c)
+            mx(o2[c][:], xq[:, P * c : P * (c + 1)], xs[:, P * c : P * (c + 1)], fq[:], fs[:])
+
+        def silu(c):
+            g, c4 = c // 4, c % 4
+            if c4 == 0:
+                rs[g] = fin_pool.tile([P, 4], F32, name="rs%d" % g, tag="rs", bufs=4)
+            axs[c] = ax_pool.tile([P, 512], BF16, name="axs%d" % c, tag="axs")
+            nc.scalar.activation(out=axs[c][:], in_=o2[c][:], func=ACT.Silu, accum_out=rs[g][:, c4 : c4 + 1])
+
+        def t_a(c0, n, b):
+            at[c0] = bank(b, [P, 1024], BF16, "at%d" % c0)
+            for j in range(n):
+                for t in range(4):
+                    nc.tensor.transpose(
+                        at[c0][:, 512 * j + P * t : 512 * j + P * (t + 1)],
+                        axs[c0 + j][:, P * t : P * (t + 1)],
+                        ident_b[:],
+                    )
+
+        def e_a(c0, n, copy):
+            g, f4 = c0 // 4, c0 % 4
+            if f4 == 0:
+                ga[g] = grp_pool.tile([P, 2048], BF16, name="ga%d" % g, tag="ga", align_bytes=64)
+            copy(
+                out=ga[g][:, 512 * f4 : 512 * (f4 + n)].rearrange("p (c b t) -> p c b t", c=n, t=4),
+                in_=at[c0][:, 0 : 512 * n].rearrange("p (c t b) -> p c b t", c=n, t=4),
+            )
+
+        def ea_engine(h):
+            if h % 2 == 1 and h >= ACT_EA_FROM and (h // 2) % ACT_EA_SKIP != ACT_EA_SKIP - 1:
+                return nc.scalar.copy
+            return nc.vector.tensor_copy
+
+        def q_a(c0, n):
+            g, f4 = c0 // 4, c0 % 4
+            axq = fin_pool.tile([P, 512], U32, name="axq%d" % c0, tag="axq", align_bytes=64)
+            axc = fin_pool.tile([P, 512], U8, name="axc%d" % c0, tag="axc", align_bytes=64)
+            quantise(axq[:, 0 : P * n], axc[:, 0 : P * n], ga[g][:, 512 * f4 : 512 * (f4 + n)])
+            unit[("axq", c0)] = axq
+            unit[("axc", c0)] = axc
+
+        def k_b(c0, n):
+            g, f4 = c0 // 4, c0 % 4
+            rsa = fin_pool.tile([P, 4], F32, name="rsa%d" % c0, tag="rsa")
+            nc.gpsimd.tensor_scalar(
+                out=rsa[:, 0:n], in0=rs[g][:, f4 : f4 + n], scalar1=na32[:, 0:1], scalar2=0.0, op0=ALU.mult, op1=ALU.add
+            )
+            kb = fin_pool.tile([P, 512], F32, name="kb%d" % c0, tag="kb")
+            nc.gpsimd.tensor_tensor(
+                out=kb[:, 0 : P * n].rearrange("p (c q) -> p c q", c=n),
+                in0=krow[:].unsqueeze(1).to_broadcast([P, n, NP]),
+                in1=rsa[:, 0:n].unsqueeze(2).to_broadcast([P, n, NP]),
+                op=ALU.add,
+            )
+            unit[("kb", c0)] = kb
+
+        def s_2(c0, n):
+            axq, axc = unit[("axq", c0)], unit[("axc", c0)]
+            ps = bank(7, [P, 512], F32, "ps%d" % c0)
+            pa = bank(5, [P, 512], F32, "pa%d" % c0)
+            pc = bank(6, [P, 512], F32, "pc%d" % c0)
+            for j in range(n):
+                c = c0 + j
+                mx(
+                    ps[:, P * j : P * (j + 1)],
+                    sxq[:, P * c : P * (c + 1)],
+                    sxs[:, P * c : P * (c + 1)],
+                    bsq[:, 0:NP],
+                    bss[:, 0:NP],
+                )
+            for j in range(n):
+                sl = slice(P * j, P * (j + 1))
+                mx(pa[:, sl], axq[:, sl], axc[:, sl], bsq[:, NP : 2 * NP], bss[:, NP : 2 * NP])
+            for j in range(n):
+                sl = slice(P * j, P * (j + 1))
+                mx(pc[:, sl], axq[:, sl], axc[:, sl], bsq[:, 0:NP], bss[:, 0:NP])
+            unit[("ps", c0)] = ps
+            unit[("pa", c0)] = pa
+            unit[("pc", c0)] = pc
+
+        def fin(c0, n):
+            kb, ps, pa, pc = unit[("kb", c0)], unit[("ps", c0)], unit[("pa", c0)], unit[("pc", c0)]
+            w = P * n
+            acc = fin_pool.tile([P, 512], F32, name="acc%d" % c0, tag="acc")
+            nc.vector.scalar_tensor_tensor(
+                out=acc[:, 0:w], in0=ps[:, 0:w], scalar=b32[:, 0:1], in1=kb[:, 0:w], op0=ALU.mult, op1=ALU.add
+            )
+            nc.vector.scalar_tensor_tensor(
+                out=acc[:, 0:w], in0=pa[:, 0:w], scalar=a32[:, 0:1], in1=acc[:, 0:w], op0=ALU.mult, op1=ALU.add
+            )
+            nc.vector.scalar_tensor_tensor(
+                out=acc[:, 0:w], in0=pc[:, 0:w], scalar=t32[:, 0:1], in1=acc[:, 0:w], op0=ALU.mult, op1=ALU.add
+            )
+            nc.sync.dma_start(out=out_rows[:, P * c0 : P * c0 + w], in_=acc[:, 0:w])
+
+        o2_pass(0)
+        o2_pass(1)
+        q_s(NG - 1)
+        nc.vector.tensor_tensor(out=bp32[:], in0=pf[:], in1=sp32[:], op=ALU.mult)
+        nc.vector.tensor_copy(
+            out=gbs[:, 0:512].rearrange("p (m t) -> p m t", t=4), in_=bp32[:].rearrange("p (t m) -> p m t", t=4)
+        )
+        nc.vector.tensor_copy(
+            out=gbs[:, 512:1024].rearrange("p (m t) -> p m t", t=4), in_=sp32[:].rearrange("p (t m) -> p m t", t=4)
+        )
+        quantise(bsq[:], bss[:], gbs[:])
+        kr = bank(5, [P, NP], F32, "kr")
+
+        for y in range(NG):
+            last = y == NG - 1
+            if y >= 1:
+                t_a(4 * y - 2, 2, 4)
+            silu(4 * y)
+            silu(4 * y + 1)
+            o2_pass(4 * y + 2)
+            o2_pass(4 * y + 3)
+            if y >= 2:
+                fin(4 * (y - 2), 4)
+            if y >= 1:
+                e_a(4 * y - 2, 2, ea_engine(2 * y - 1))
+            t_a(4 * y, 2, 3)
+            if y >= 1:
+                q_a(4 * (y - 1), 4)
+            silu(4 * y + 2)
+            silu(4 * y + 3)
+            if not last:
+                o2_pass(4 * y + 4)
+                o2_pass(4 * y + 5)
+            if y == 0:
+                for t in range(4):
+                    nc.tensor.matmul(
+                        kr[:], lhsT=ones_f[:], rhs=bp32[:, P * t : P * (t + 1)], start=(t == 0), stop=(t == 3)
+                    )
+            if y >= 1:
+                k_b(4 * (y - 1), 4)
+                s_2(4 * (y - 1), 4)
+            e_a(4 * y, 2, ea_engine(2 * y))
+            if y == 0:
+                nc.vector.tensor_scalar_mul(out=krow[:], in0=kr[:], scalar1=nb32[:, 0:1])
+
+        c0 = NCH - 4
+        t_a(c0 + 2, 1, 4)
+        t_a(c0 + 3, 1, 3)
+        e_a(c0 + 2, 1, nc.scalar.copy)
+        q_a(c0, 2)
+        e_a(c0 + 3, 1, nc.vector.tensor_copy)
+        k_b(c0, 2)
+        k_b(c0 + 2, 2)
+        fin(c0 - 4, 4)
+        s_2(c0, 2)
+        q_a(c0 + 2, 2)
+        fin(c0, 2)
+        s_2(c0 + 2, 2)
+        fin(c0 + 2, 2)

@@ -21,6 +21,7 @@ FLOPS = 2 * (B + NP) * D * F + 3 * 2 * B * F * NP
 ACT_EA_FROM = 1
 ACT_EA_SKIP = 99
 HEAD_ACT_E = 1
+AT_ODD, AT_EVEN = 4, 3
 
 
 def tile_tverskylayer_pa_t_kernel(tc, x, features, prototypes, alpha, beta, theta, out):
@@ -56,6 +57,9 @@ def tile_tverskylayer_pa_t_kernel(tc, x, features, prototypes, alpha, beta, thet
         t_bf = const.tile([P, 1], BF16, name="t_bf")
         gf = const.tile([P, 4 * F], BF16, name="gf", align_bytes=64)
         gp = const.tile([P, 4 * NP], BF16, name="gp", align_bytes=64)
+        gf2 = const.tile([P, 4 * F], BF16, name="gf2", align_bytes=64)
+        fq2 = const.tile([P, F], U32, name="fq2", align_bytes=64)
+        fs2 = const.tile([P, F], U8, name="fs2", align_bytes=64)
         fq = const.tile([P, F], U32, name="fq", align_bytes=64)
         fs = const.tile([P, F], U8, name="fs", align_bytes=64)
         pq = const.tile([P, NP], U32, name="pq", align_bytes=64)
@@ -144,6 +148,7 @@ def tile_tverskylayer_pa_t_kernel(tc, x, features, prototypes, alpha, beta, thet
         t_x(0)
         load_x(6)
         quantise(fq[:], fs[:], gf[:])
+
         e_x(0, 0, nc.scalar.copy if HEAD_ACT_E else nc.vector.tensor_copy)
         t_x(1)
         load_x(7)
@@ -208,6 +213,13 @@ def tile_tverskylayer_pa_t_kernel(tc, x, features, prototypes, alpha, beta, thet
                 nc.vector.tensor_scalar_mul(out=na32[:], in0=a32[:], scalar1=-1.0)
                 nc.vector.tensor_scalar_mul(out=nb32[:], in0=b32[:], scalar1=-1.0)
                 quantise(pq[:], pscl[:], gp[:])
+                gf2w = gf2[:].bitcast(F32)
+                for j in range(2):
+                    nc.vector.tensor_copy(
+                        out=gf2w[:, 512 * j : 512 * (j + 1)].rearrange("p (m e u) -> p m e u", e=2, u=2),
+                        in_=gfw[:, 512 * j : 512 * (j + 1)].rearrange("p (e m u) -> p m e u", e=2, u=2),
+                    )
+                quantise(fq2[:], fs2[:], gf2[:])
 
         pf = bank(3, [P, 512], F32, "pf")
         for t in range(4):
@@ -223,7 +235,7 @@ def tile_tverskylayer_pa_t_kernel(tc, x, features, prototypes, alpha, beta, thet
 
         def o2_pass(c):
             o2[c] = bank(c % 3, [P, 512], F32, "o2_%d" % c)
-            mx(o2[c][:], xq[:, P * c : P * (c + 1)], xs[:, P * c : P * (c + 1)], fq[:], fs[:])
+            mx(o2[c][:], xq[:, P * c : P * (c + 1)], xs[:, P * c : P * (c + 1)], fq2[:], fs2[:])
 
         def silu(c):
             g, c4 = c // 4, c % 4
@@ -233,23 +245,20 @@ def tile_tverskylayer_pa_t_kernel(tc, x, features, prototypes, alpha, beta, thet
             nc.scalar.activation(out=axs[c][:], in_=o2[c][:], func=ACT.Silu, accum_out=rs[g][:, c4 : c4 + 1])
 
         def t_a(c0, n, b):
-            at[c0] = bank(b, [P, 1024], BF16, "at%d" % c0)
+            at[c0] = bank(b, [P, 512], F32, "at%d" % c0)
             for j in range(n):
-                for t in range(4):
+                for u in range(2):
                     nc.tensor.transpose(
-                        at[c0][:, 512 * j + P * t : 512 * j + P * (t + 1)],
-                        axs[c0 + j][:, P * t : P * (t + 1)],
-                        ident_b[:],
+                        at[c0][:, 256 * j + P * u : 256 * j + P * (u + 1)],
+                        axs[c0 + j][:].bitcast(F32)[:, P * u : P * (u + 1)],
+                        ident_f[:],
                     )
 
         def e_a(c0, n, copy):
             g, f4 = c0 // 4, c0 % 4
             if f4 == 0:
                 ga[g] = grp_pool.tile([P, 2048], BF16, name="ga%d" % g, tag="ga", align_bytes=64)
-            copy(
-                out=ga[g][:, 512 * f4 : 512 * (f4 + n)].rearrange("p (c b t) -> p c b t", c=n, t=4),
-                in_=at[c0][:, 0 : 512 * n].rearrange("p (c t b) -> p c b t", c=n, t=4),
-            )
+            exit_words(copy, ga[g][:].bitcast(F32), f4, n, at[c0])
 
         def ea_engine(h):
             if h % 2 == 1 and h >= ACT_EA_FROM and (h // 2) % ACT_EA_SKIP != ACT_EA_SKIP - 1:
@@ -334,16 +343,19 @@ def tile_tverskylayer_pa_t_kernel(tc, x, features, prototypes, alpha, beta, thet
         for y in range(NG):
             last = y == NG - 1
             if y >= 1:
-                t_a(4 * y - 2, 2, 4)
+                t_a(4 * y - 2, 2, AT_ODD)
             silu(4 * y)
             silu(4 * y + 1)
             o2_pass(4 * y + 2)
             o2_pass(4 * y + 3)
             if y >= 2:
-                fin(4 * (y - 2), 4)
+                k_b(4 * (y - 2), 4)
+                s_2(4 * (y - 2), 4)
             if y >= 1:
                 e_a(4 * y - 2, 2, ea_engine(2 * y - 1))
-            t_a(4 * y, 2, 3)
+            t_a(4 * y, 2, AT_EVEN)
+            if y >= 2:
+                fin(4 * (y - 2), 4)
             if y >= 1:
                 q_a(4 * (y - 1), 4)
             silu(4 * y + 2)
@@ -356,24 +368,23 @@ def tile_tverskylayer_pa_t_kernel(tc, x, features, prototypes, alpha, beta, thet
                     nc.tensor.matmul(
                         kr[:], lhsT=ones_f[:], rhs=bp32[:, P * t : P * (t + 1)], start=(t == 0), stop=(t == 3)
                     )
-            if y >= 1:
-                k_b(4 * (y - 1), 4)
-                s_2(4 * (y - 1), 4)
             e_a(4 * y, 2, ea_engine(2 * y))
             if y == 0:
                 nc.vector.tensor_scalar_mul(out=krow[:], in0=kr[:], scalar1=nb32[:, 0:1])
 
         c0 = NCH - 4
-        t_a(c0 + 2, 1, 4)
-        t_a(c0 + 3, 1, 3)
+        t_a(c0 + 2, 1, 0)
+        t_a(c0 + 3, 1, 1)
+        k_b(c0 - 4, 4)
+        s_2(c0 - 4, 4)
         e_a(c0 + 2, 1, nc.scalar.copy)
+        e_a(c0 + 3, 1, nc.scalar.copy)
         q_a(c0, 2)
-        e_a(c0 + 3, 1, nc.vector.tensor_copy)
-        k_b(c0, 2)
-        k_b(c0 + 2, 2)
         fin(c0 - 4, 4)
+        k_b(c0, 2)
         s_2(c0, 2)
         q_a(c0 + 2, 2)
         fin(c0, 2)
+        k_b(c0 + 2, 2)
         s_2(c0 + 2, 2)
         fin(c0 + 2, 2)

@@ -196,10 +196,14 @@ def tile_tverskylayer_pa_t_kernel(tc, x, features, prototypes, alpha, beta, thet
             if i == NG - 2:
                 pt = bank(0, [P, 512], F32, "pt")
                 word_transposes(p_sb[:].bitcast(F32), 0, 1, pt)
+            act_e = i + 2 < NG and (i + 2) % 4 == 0
             for c4 in range(4):
                 o1_sig(4 * i + c4)
+                if c4 == 1 and act_e:
+                    e_x(i + 2, 0, nc.scalar.copy)
             if i + 2 < NG:
-                e_x(i + 2, 0, nc.vector.tensor_copy)
+                if not act_e:
+                    e_x(i + 2, 0, nc.vector.tensor_copy)
                 e_x(i + 2, 1, nc.vector.tensor_copy)
             if i >= 1:
                 q_s(i - 1)
@@ -288,11 +292,11 @@ def tile_tverskylayer_pa_t_kernel(tc, x, features, prototypes, alpha, beta, thet
             )
             unit[("kb", c0)] = kb
 
-        def s_2(c0, n):
+        def s_2(c0, n, banks=(7, 5, 6)):
             axq, axc = unit[("axq", c0)], unit[("axc", c0)]
-            ps = bank(7, [P, 512], F32, "ps%d" % c0)
-            pa = bank(5, [P, 512], F32, "pa%d" % c0)
-            pc = bank(6, [P, 512], F32, "pc%d" % c0)
+            ps = bank(banks[0], [P, 512], F32, "ps%d" % c0)
+            pa = bank(banks[1], [P, 512], F32, "pa%d" % c0)
+            pc = bank(banks[2], [P, 512], F32, "pc%d" % c0)
             for j in range(n):
                 c = c0 + j
                 mx(
@@ -312,20 +316,38 @@ def tile_tverskylayer_pa_t_kernel(tc, x, features, prototypes, alpha, beta, thet
             unit[("pa", c0)] = pa
             unit[("pc", c0)] = pc
 
-        def fin(c0, n):
-            kb, ps, pa, pc = unit[("kb", c0)], unit[("ps", c0)], unit[("pa", c0)], unit[("pc", c0)]
+        def fin_s(c0, n):
             w = P * n
             acc = fin_pool.tile([P, 512], F32, name="acc%d" % c0, tag="acc")
+            unit[("acc", c0)] = acc
             nc.vector.scalar_tensor_tensor(
-                out=acc[:, 0:w], in0=ps[:, 0:w], scalar=b32[:, 0:1], in1=kb[:, 0:w], op0=ALU.mult, op1=ALU.add
+                out=acc[:, 0:w],
+                in0=unit[("ps", c0)][:, 0:w],
+                scalar=b32[:, 0:1],
+                in1=unit[("kb", c0)][:, 0:w],
+                op0=ALU.mult,
+                op1=ALU.add,
             )
+
+        def fin_a(c0, n):
+            w = P * n
+            acc = unit[("acc", c0)]
             nc.vector.scalar_tensor_tensor(
-                out=acc[:, 0:w], in0=pa[:, 0:w], scalar=a32[:, 0:1], in1=acc[:, 0:w], op0=ALU.mult, op1=ALU.add
+                out=acc[:, 0:w], in0=unit[("pa", c0)][:, 0:w], scalar=a32[:, 0:1], in1=acc[:, 0:w], op0=ALU.mult, op1=ALU.add
             )
+
+        def fin_c(c0, n):
+            w = P * n
+            acc = unit[("acc", c0)]
             nc.vector.scalar_tensor_tensor(
-                out=acc[:, 0:w], in0=pc[:, 0:w], scalar=t32[:, 0:1], in1=acc[:, 0:w], op0=ALU.mult, op1=ALU.add
+                out=acc[:, 0:w], in0=unit[("pc", c0)][:, 0:w], scalar=t32[:, 0:1], in1=acc[:, 0:w], op0=ALU.mult, op1=ALU.add
             )
             nc.sync.dma_start(out=out_rows[:, P * c0 : P * c0 + w], in_=acc[:, 0:w])
+
+        def fin(c0, n):
+            fin_s(c0, n)
+            fin_a(c0, n)
+            fin_c(c0, n)
 
         o2_pass(0)
         o2_pass(1)
@@ -355,9 +377,11 @@ def tile_tverskylayer_pa_t_kernel(tc, x, features, prototypes, alpha, beta, thet
                 e_a(4 * y - 2, 2, ea_engine(2 * y - 1))
             t_a(4 * y, 2, AT_EVEN)
             if y >= 2:
-                fin(4 * (y - 2), 4)
+                fin_s(4 * (y - 2), 4)
             if y >= 1:
                 q_a(4 * (y - 1), 4)
+            if y >= 2:
+                fin_a(4 * (y - 2), 4)
             silu(4 * y + 2)
             silu(4 * y + 3)
             if not last:
@@ -368,23 +392,31 @@ def tile_tverskylayer_pa_t_kernel(tc, x, features, prototypes, alpha, beta, thet
                     nc.tensor.matmul(
                         kr[:], lhsT=ones_f[:], rhs=bp32[:, P * t : P * (t + 1)], start=(t == 0), stop=(t == 3)
                     )
-            e_a(4 * y, 2, ea_engine(2 * y))
+            e_a(4 * y, 2, nc.scalar.copy if last else ea_engine(2 * y))
+            if y >= 2:
+                fin_c(4 * (y - 2), 4)
             if y == 0:
                 nc.vector.tensor_scalar_mul(out=krow[:], in0=kr[:], scalar1=nb32[:, 0:1])
 
         c0 = NCH - 4
-        t_a(c0 + 2, 1, 0)
-        t_a(c0 + 3, 1, 1)
+        t_a(c0 + 2, 1, 1)
+        t_a(c0 + 3, 1, 2)
         k_b(c0 - 4, 4)
         s_2(c0 - 4, 4)
         e_a(c0 + 2, 1, nc.scalar.copy)
         e_a(c0 + 3, 1, nc.scalar.copy)
+        fin_s(c0 - 4, 4)
         q_a(c0, 2)
-        fin(c0 - 4, 4)
+        fin_a(c0 - 4, 4)
         k_b(c0, 2)
-        s_2(c0, 2)
+        s_2(c0, 2, (0, 3, 4))
         q_a(c0 + 2, 2)
-        fin(c0, 2)
+        fin_c(c0 - 4, 4)
         k_b(c0 + 2, 2)
         s_2(c0 + 2, 2)
-        fin(c0 + 2, 2)
+        fin_s(c0, 2)
+        fin_s(c0 + 2, 2)
+        fin_a(c0, 2)
+        fin_a(c0 + 2, 2)
+        fin_c(c0, 2)
+        fin_c(c0 + 2, 2)

@@ -15,13 +15,15 @@ P = 128
 B, D, F, NP = 8192, 512, 512, 128
 NCH = B // P
 NG = NCH // 4
-NH = NCH // 2
 FLOPS = 2 * (B + NP) * D * F + 3 * 2 * B * F * NP
 
-ACT_EA_FROM = 1
-ACT_EA_SKIP = 99
-HEAD_ACT_E = 1
-AT_ODD, AT_EVEN = 4, 3
+XT_BANKS = (0, 1, 2)
+O2_BANKS = (3, 4, 5)
+AT_BANKS = (6, 7)
+O1_BANKS = (0, 3, 4, 5)
+PS_BANKS = (1, 2)
+PA_BANK = 6
+PC_BANK = 7
 
 
 def tile_tverskylayer_pa_t_kernel(tc, x, features, prototypes, alpha, beta, theta, out):
@@ -43,57 +45,43 @@ def tile_tverskylayer_pa_t_kernel(tc, x, features, prototypes, alpha, beta, thet
 
         ident_f = const.tile([P, P], F32, name="ident_f")
         make_identity(nc, ident_f[:])
-        ident_b = const.tile([P, P], BF16, name="ident_b")
-        make_identity(nc, ident_b[:])
         ones_f = const.tile([P, P], F32, name="ones_f")
         nc.vector.memset(ones_f[:], 1.0)
         warm = const.tile([P, 1], F32, name="warm")
-        nc.scalar.activation(out=warm[:], in_=ones_f[:, 0:1], func=ACT.Sigmoid)
+        nc.scalar.activation(out=warm[:], in_=ones_f[:, 0:1], func=ACT.Silu)
 
         f_sb = const.tile([P, 4 * D], BF16, name="f_sb")
         p_sb = const.tile([P, D], BF16, name="p_sb")
         a_bf = const.tile([P, 1], BF16, name="a_bf")
         b_bf = const.tile([P, 1], BF16, name="b_bf")
         t_bf = const.tile([P, 1], BF16, name="t_bf")
-        gf = const.tile([P, 4 * F], BF16, name="gf", align_bytes=64)
-        gp = const.tile([P, 4 * NP], BF16, name="gp", align_bytes=64)
+        gf1 = const.tile([P, 4 * F], BF16, name="gf1", align_bytes=64)
         gf2 = const.tile([P, 4 * F], BF16, name="gf2", align_bytes=64)
+        gp = const.tile([P, 4 * NP], BF16, name="gp", align_bytes=64)
+        fq1 = const.tile([P, F], U32, name="fq1", align_bytes=64)
+        fs1 = const.tile([P, F], U8, name="fs1", align_bytes=64)
         fq2 = const.tile([P, F], U32, name="fq2", align_bytes=64)
         fs2 = const.tile([P, F], U8, name="fs2", align_bytes=64)
-        fq = const.tile([P, F], U32, name="fq", align_bytes=64)
-        fs = const.tile([P, F], U8, name="fs", align_bytes=64)
         pq = const.tile([P, NP], U32, name="pq", align_bytes=64)
         pscl = const.tile([P, NP], U8, name="pscl", align_bytes=64)
         xq = const.tile([P, B], U32, name="xq", align_bytes=64)
         xs = const.tile([P, B], U8, name="xs", align_bytes=64)
-        sxq = const.tile([P, B], U32, name="sxq", align_bytes=64)
-        sxs = const.tile([P, B], U8, name="sxs", align_bytes=64)
-        sp32 = const.tile([P, F], F32, name="sp32")
+        axq = const.tile([P, B], U32, name="axq", align_bytes=64)
+        axc = const.tile([P, B], U8, name="axc", align_bytes=64)
+        rs = const.tile([P, NCH], F32, name="rs")
         bp32 = const.tile([P, F], F32, name="bp32")
-        gbs = const.tile([P, 8 * NP], BF16, name="gbs", align_bytes=64)
-        bsq = const.tile([P, 2 * NP], U32, name="bsq", align_bytes=64)
-        bss = const.tile([P, 2 * NP], U8, name="bss", align_bytes=64)
+        gbp = const.tile([P, 4 * NP], BF16, name="gbp", align_bytes=64)
+        gsp = const.tile([P, 4 * NP], BF16, name="gsp", align_bytes=64)
+        bpq = const.tile([P, NP], U32, name="bpq", align_bytes=64)
+        bpc = const.tile([P, NP], U8, name="bpc", align_bytes=64)
+        spq = const.tile([P, NP], U32, name="spq", align_bytes=64)
+        spc = const.tile([P, NP], U8, name="spc", align_bytes=64)
         krow = const.tile([P, NP], F32, name="krow")
         a32 = const.tile([P, 1], F32, name="a32")
         b32 = const.tile([P, 1], F32, name="b32")
         t32 = const.tile([P, 1], F32, name="t32")
         na32 = const.tile([P, 1], F32, name="na32")
         nb32 = const.tile([P, 1], F32, name="nb32")
-
-        xin = {}
-
-        def load_x(g, pieces=1):
-            xin[g] = xin_pool.tile([P, 4 * D], BF16, name="xin%d" % g, tag="xin")
-            w = 4 * D // pieces
-            for k in range(pieces):
-                nc.sync.dma_start(
-                    out=xin[g][:, w * k : w * (k + 1)], in_=x_rows[:, 4 * D * g + w * k : 4 * D * g + w * (k + 1)]
-                )
-
-        nc.sync.dma_start(out=f_sb[:], in_=features.rearrange("(p t) d -> p (t d)", t=4))
-        load_x(0, pieces=2)
-        for g in range(1, 6):
-            load_x(g)
 
         def word_transposes(src_words, first_chunk, n_chunks, pbank):
             for j in range(n_chunks):
@@ -120,14 +108,24 @@ def tile_tverskylayer_pa_t_kernel(tc, x, features, prototypes, alpha, beta, thet
                 out=o, lhsT=l.bitcast(FP8X4), lhsT_scale=ls, rhs=r.bitcast(FP8X4), rhs_scale=rs_, start=True, stop=True
             )
 
+        def cols(i, w=P):
+            return slice(w * i, w * (i + 1))
+
+        xin = {}
         xt = {}
         gx = {}
 
-        def t_x(g):
-            xw = xin[g][:].bitcast(F32)
-            for k in range(2):
-                xt[(g, k)] = bank((2 * g + k) % 4, [P, 512], F32, "xt%d_%d" % (g, k))
-                word_transposes(xw, 2 * k, 2, xt[(g, k)])
+        def load_x(g, pieces=1):
+            xin[g] = xin_pool.tile([P, 4 * D], BF16, name="xin%d" % g, tag="xin")
+            w = 4 * D // pieces
+            for k in range(pieces):
+                nc.sync.dma_start(
+                    out=xin[g][:, w * k : w * (k + 1)], in_=x_rows[:, 4 * D * g + w * k : 4 * D * g + w * (k + 1)]
+                )
+
+        def t_x(g, k):
+            xt[(g, k)] = bank(XT_BANKS[(2 * g + k) % 3], [P, 512], F32, "xt%d_%d" % (g, k))
+            word_transposes(xin[g][:].bitcast(F32), 2 * k, 2, xt[(g, k)])
 
         def e_x(g, k, copy):
             if k == 0:
@@ -138,285 +136,248 @@ def tile_tverskylayer_pa_t_kernel(tc, x, features, prototypes, alpha, beta, thet
             lo, hi = 512 * g + P * first, 512 * g + P * (first + n)
             quantise(xq[:, lo:hi], xs[:, lo:hi], gx[g][:, 512 * first : 512 * (first + n)])
 
-        fw = f_sb[:].bitcast(F32)
-        gfw = gf[:].bitcast(F32)
-        ft = [bank(4 + j, [P, 512], F32, "ft%d" % j) for j in range(2)]
-        for j in range(2):
-            word_transposes(fw, 2 * j, 2, ft[j])
-        exit_words(nc.vector.tensor_copy, gfw, 0, 2, ft[0])
-        exit_words(nc.scalar.copy, gfw, 2, 2, ft[1])
-        t_x(0)
-        load_x(6)
-        quantise(fq[:], fs[:], gf[:])
+        o2 = {}
+        axs = {}
+        at = {}
+        ga = {}
 
-        e_x(0, 0, nc.scalar.copy if HEAD_ACT_E else nc.vector.tensor_copy)
-        t_x(1)
+        def o2_pass(c):
+            o2[c] = bank(O2_BANKS[c % 3], [P, 512], F32, "o2_%d" % c)
+            mx(o2[c][:], xq[:, cols(c)], xs[:, cols(c)], fq2[:], fs2[:])
+
+        def silu(c):
+            axs[c] = ax_pool.tile([P, 512], BF16, name="axs%d" % c, tag="axs")
+            nc.scalar.activation(out=axs[c][:], in_=o2[c][:], func=ACT.Silu, accum_out=rs[:, c : c + 1])
+
+        def t_a(h):
+            at[h] = bank(AT_BANKS[h % 2], [P, 512], F32, "at%d" % h)
+            for j in range(2):
+                word_transposes(axs[2 * h + j][:].bitcast(F32), 0, 1, at[h][:, 256 * j : 256 * (j + 1)])
+
+        def e_a(h, copy):
+            g, k = h // 2, h % 2
+            if k == 0:
+                ga[g] = grp_pool.tile([P, 2048], BF16, name="ga%d" % g, tag="ga", align_bytes=64)
+            exit_words(copy, ga[g][:].bitcast(F32), 2 * k, 2, at[h])
+
+        def q_a(g):
+            quantise(axq[:, cols(g, 512)], axc[:, cols(g, 512)], ga[g][:])
+
+        nc.sync.dma_start(out=f_sb[:], in_=features.rearrange("(p t) d -> p (t d)", t=4))
+        load_x(0, pieces=2)
+        for g in range(1, 6):
+            load_x(g)
+        gf1w = gf1[:].bitcast(F32)
+        gf2w = gf2[:].bitcast(F32)
+        ft = [bank(O2_BANKS[j], [P, 512], F32, "ft%d" % j) for j in range(2)]
+        for j in range(2):
+            word_transposes(f_sb[:].bitcast(F32), 2 * j, 2, ft[j])
+        for j, copy in ((0, nc.vector.tensor_copy), (1, nc.scalar.copy)):
+            copy(
+                out=gf2w[:, cols(j, 512)].rearrange("p (m e u) -> p m e u", e=2, u=2),
+                in_=ft[j][:].rearrange("p (e u m) -> p m e u", e=2, u=2),
+            )
+        t_x(0, 0)
+        t_x(0, 1)
+        load_x(6)
+        quantise(fq2[:], fs2[:], gf2[:])
+        e_x(0, 0, nc.scalar.copy)
+        t_x(1, 0)
+        t_x(1, 1)
         load_x(7)
         e_x(0, 1, nc.vector.tensor_copy)
         q_x(0, 0, 2)
         e_x(1, 0, nc.vector.tensor_copy)
         q_x(0, 2, 2)
         e_x(1, 1, nc.vector.tensor_copy)
-        q_x(1)
+        o2_pass(0)
+        o2_pass(1)
 
-        gs = {}
-
-        def o1_sig(c):
-            g, c4 = c // 4, c % 4
-            if c4 == 0:
-                gs[g] = grp_pool.tile([P, 2048], BF16, name="gs%d" % g, tag="gs", align_bytes=64)
-            o1 = bank(4 + c4, [P, 512], F32, "o1_%d" % c)
-            for t in range(4):
-                mx(
-                    o1[:, P * t : P * (t + 1)],
-                    fq[:, P * t : P * (t + 1)],
-                    fs[:, P * t : P * (t + 1)],
-                    xq[:, P * c : P * (c + 1)],
-                    xs[:, P * c : P * (c + 1)],
-                )
-            nc.scalar.activation(
-                out=gs[g][:, 512 * c4 : 512 * (c4 + 1)].rearrange("p (b t) -> p b t", t=4),
-                in_=o1[:].rearrange("p (t b) -> p b t", t=4),
-                func=ACT.Sigmoid,
-            )
-
-        def q_s(g):
-            quantise(sxq[:, 512 * g : 512 * (g + 1)], sxs[:, 512 * g : 512 * (g + 1)], gs[g][:])
-
-        for i in range(NG):
-            if i + 2 < NG:
-                t_x(i + 2)
-            if i + 8 < NG:
-                load_x(i + 8)
-            if i == 8:
+        for y in range(NG):
+            more_x = y + 2 < NG
+            if y >= 1:
+                t_a(2 * y - 1)
+            if more_x:
+                t_x(y + 2, 0)
+            if y == NG - 2:
+                pt = bank(XT_BANKS[0], [P, 512], F32, "pt")
+                word_transposes(p_sb[:].bitcast(F32), 0, 1, pt)
+            silu(4 * y)
+            silu(4 * y + 1)
+            o2_pass(4 * y + 2)
+            o2_pass(4 * y + 3)
+            if y >= 1:
+                e_a(2 * y - 2, nc.vector.tensor_copy)
+            if y + 1 < NG:
+                q_x(y + 1)
+            if y >= 1:
+                e_a(2 * y - 1, nc.scalar.copy)
+            if more_x:
+                e_x(y + 2, 0, nc.vector.tensor_copy)
+            t_a(2 * y)
+            if more_x:
+                t_x(y + 2, 1)
+            if y + 8 < NG:
+                load_x(y + 8)
+            if y == 8:
                 nc.sync.dma_start(out=p_sb[:], in_=prototypes)
                 nc.sync.dma_start(out=a_bf[:], in_=alpha.partition_broadcast(P))
                 nc.sync.dma_start(out=b_bf[:], in_=beta.partition_broadcast(P))
                 nc.sync.dma_start(out=t_bf[:], in_=theta.partition_broadcast(P))
-            if i == NG - 2:
-                pt = bank(0, [P, 512], F32, "pt")
-                word_transposes(p_sb[:].bitcast(F32), 0, 1, pt)
-            act_e = i + 2 < NG and (i + 2) % 4 == 0
-            for c4 in range(4):
-                o1_sig(4 * i + c4)
-                if c4 == 1 and act_e:
-                    e_x(i + 2, 0, nc.scalar.copy)
-            if i + 2 < NG:
-                if not act_e:
-                    e_x(i + 2, 0, nc.vector.tensor_copy)
-                e_x(i + 2, 1, nc.vector.tensor_copy)
-            if i >= 1:
-                q_s(i - 1)
-            if i + 2 < NG:
-                q_x(i + 2)
-            if i == NG - 2:
+            if y >= 2:
+                q_a(y - 2)
+            if y == NG - 1:
+                pf = bank(XT_BANKS[1], [P, 512], F32, "pf")
+                for t in range(4):
+                    mx(pf[:, cols(t)], fq1[:, cols(t)], fs1[:, cols(t)], pq[:], pscl[:])
+                nc.scalar.activation(out=bp32[:], in_=pf[:], func=ACT.Silu)
+            silu(4 * y + 2)
+            silu(4 * y + 3)
+            if y + 1 < NG:
+                o2_pass(4 * y + 4)
+                o2_pass(4 * y + 5)
+            if more_x:
+                e_x(y + 2, 1, nc.vector.tensor_copy)
+            if y == NG - 2:
                 exit_words(nc.vector.tensor_copy, gp[:].bitcast(F32), 0, 1, pt)
+                for j in range(2):
+                    nc.vector.tensor_copy(
+                        out=gf1w[:, cols(j, 512)].rearrange("p (e m u) -> p e m u", e=2, u=2),
+                        in_=gf2w[:, cols(j, 512)].rearrange("p (m e u) -> p e m u", e=2, u=2),
+                    )
+                quantise(pq[:], pscl[:], gp[:])
+                quantise(fq1[:], fs1[:], gf1[:])
                 nc.vector.tensor_copy(out=a32[:], in_=a_bf[:])
                 nc.vector.tensor_copy(out=b32[:], in_=b_bf[:])
                 nc.vector.tensor_copy(out=t32[:], in_=t_bf[:])
                 nc.vector.tensor_scalar_mul(out=na32[:], in0=a32[:], scalar1=-1.0)
                 nc.vector.tensor_scalar_mul(out=nb32[:], in0=b32[:], scalar1=-1.0)
-                quantise(pq[:], pscl[:], gp[:])
-                gf2w = gf2[:].bitcast(F32)
-                for j in range(2):
-                    nc.vector.tensor_copy(
-                        out=gf2w[:, 512 * j : 512 * (j + 1)].rearrange("p (m e u) -> p m e u", e=2, u=2),
-                        in_=gfw[:, 512 * j : 512 * (j + 1)].rearrange("p (e m u) -> p m e u", e=2, u=2),
-                    )
-                quantise(fq2[:], fs2[:], gf2[:])
+            if y == NG - 1:
+                kr = bank(XT_BANKS[2], [P, NP], F32, "kr")
+                for t in range(4):
+                    nc.tensor.matmul(kr[:], lhsT=ones_f[:], rhs=bp32[:, cols(t)], start=(t == 0), stop=(t == 3))
+                nc.vector.tensor_copy(
+                    out=gbp[:].rearrange("p (m t) -> p m t", t=4), in_=bp32[:].rearrange("p (t m) -> p m t", t=4)
+                )
+                nc.vector.tensor_scalar_mul(out=krow[:], in0=kr[:], scalar1=nb32[:, 0:1])
+                quantise(bpq[:], bpc[:], gbp[:])
 
-        pf = bank(3, [P, 512], F32, "pf")
-        for t in range(4):
-            mx(pf[:, P * t : P * (t + 1)], fq[:, P * t : P * (t + 1)], fs[:, P * t : P * (t + 1)], pq[:], pscl[:])
-        nc.scalar.activation(out=sp32[:], in_=pf[:], func=ACT.Sigmoid)
-
-        o2 = {}
-        axs = {}
-        rs = {}
-        at = {}
-        ga = {}
+        o1 = {}
+        gs = {}
         unit = {}
 
-        def o2_pass(c):
-            o2[c] = bank(c % 3, [P, 512], F32, "o2_%d" % c)
-            mx(o2[c][:], xq[:, P * c : P * (c + 1)], xs[:, P * c : P * (c + 1)], fq2[:], fs2[:])
+        def o1_pass(c):
+            o1[c] = bank(O1_BANKS[c % 4], [P, 512], F32, "o1_%d" % c)
+            for t in range(4):
+                mx(o1[c][:, cols(t)], fq1[:, cols(t)], fs1[:, cols(t)], xq[:, cols(c)], xs[:, cols(c)])
 
-        def silu(c):
+        def sigmoid(c):
             g, c4 = c // 4, c % 4
             if c4 == 0:
-                rs[g] = fin_pool.tile([P, 4], F32, name="rs%d" % g, tag="rs", bufs=4)
-            axs[c] = ax_pool.tile([P, 512], BF16, name="axs%d" % c, tag="axs")
-            nc.scalar.activation(out=axs[c][:], in_=o2[c][:], func=ACT.Silu, accum_out=rs[g][:, c4 : c4 + 1])
-
-        def t_a(c0, n, b):
-            at[c0] = bank(b, [P, 512], F32, "at%d" % c0)
-            for j in range(n):
-                for u in range(2):
-                    nc.tensor.transpose(
-                        at[c0][:, 256 * j + P * u : 256 * j + P * (u + 1)],
-                        axs[c0 + j][:].bitcast(F32)[:, P * u : P * (u + 1)],
-                        ident_f[:],
-                    )
-
-        def e_a(c0, n, copy):
-            g, f4 = c0 // 4, c0 % 4
-            if f4 == 0:
-                ga[g] = grp_pool.tile([P, 2048], BF16, name="ga%d" % g, tag="ga", align_bytes=64)
-            exit_words(copy, ga[g][:].bitcast(F32), f4, n, at[c0])
-
-        def ea_engine(h):
-            if h % 2 == 1 and h >= ACT_EA_FROM and (h // 2) % ACT_EA_SKIP != ACT_EA_SKIP - 1:
-                return nc.scalar.copy
-            return nc.vector.tensor_copy
-
-        def q_a(c0, n):
-            g, f4 = c0 // 4, c0 % 4
-            axq = fin_pool.tile([P, 512], U32, name="axq%d" % c0, tag="axq", align_bytes=64)
-            axc = fin_pool.tile([P, 512], U8, name="axc%d" % c0, tag="axc", align_bytes=64)
-            quantise(axq[:, 0 : P * n], axc[:, 0 : P * n], ga[g][:, 512 * f4 : 512 * (f4 + n)])
-            unit[("axq", c0)] = axq
-            unit[("axc", c0)] = axc
-
-        def k_b(c0, n):
-            g, f4 = c0 // 4, c0 % 4
-            rsa = fin_pool.tile([P, 4], F32, name="rsa%d" % c0, tag="rsa")
-            nc.gpsimd.tensor_scalar(
-                out=rsa[:, 0:n], in0=rs[g][:, f4 : f4 + n], scalar1=na32[:, 0:1], scalar2=0.0, op0=ALU.mult, op1=ALU.add
+                gs[g] = grp_pool.tile([P, 2048], BF16, name="gs%d" % g, tag="gs", align_bytes=64)
+            nc.scalar.activation(
+                out=gs[g][:, cols(c4, 512)].rearrange("p (b t) -> p b t", t=4),
+                in_=o1[c][:].rearrange("p (t b) -> p b t", t=4),
+                func=ACT.Sigmoid,
             )
-            kb = fin_pool.tile([P, 512], F32, name="kb%d" % c0, tag="kb")
+
+        def q_s(g):
+            sxq = fin_pool.tile([P, 512], U32, name="sxq%d" % g, tag="sxq", align_bytes=64)
+            sxc = fin_pool.tile([P, 512], U8, name="sxc%d" % g, tag="sxc", align_bytes=64)
+            quantise(sxq[:], sxc[:], gs[g][:])
+            unit[("sxq", g)] = sxq
+            unit[("sxc", g)] = sxc
+
+        def k_b(g):
+            rsa = fin_pool.tile([P, 4], F32, name="rsa%d" % g, tag="rsa")
+            nc.gpsimd.tensor_scalar(
+                out=rsa[:], in0=rs[:, cols(g, 4)], scalar1=na32[:, 0:1], scalar2=0.0, op0=ALU.mult, op1=ALU.add
+            )
+            kb = fin_pool.tile([P, 512], F32, name="kb%d" % g, tag="kb")
             nc.gpsimd.tensor_tensor(
-                out=kb[:, 0 : P * n].rearrange("p (c q) -> p c q", c=n),
-                in0=krow[:].unsqueeze(1).to_broadcast([P, n, NP]),
-                in1=rsa[:, 0:n].unsqueeze(2).to_broadcast([P, n, NP]),
+                out=kb[:].rearrange("p (c q) -> p c q", c=4),
+                in0=krow[:].unsqueeze(1).to_broadcast([P, 4, NP]),
+                in1=rsa[:].unsqueeze(2).to_broadcast([P, 4, NP]),
                 op=ALU.add,
             )
-            unit[("kb", c0)] = kb
+            unit[("kb", g)] = kb
 
-        def s_2(c0, n, banks=(7, 5, 6)):
-            axq, axc = unit[("axq", c0)], unit[("axc", c0)]
-            ps = bank(banks[0], [P, 512], F32, "ps%d" % c0)
-            pa = bank(banks[1], [P, 512], F32, "pa%d" % c0)
-            pc = bank(banks[2], [P, 512], F32, "pc%d" % c0)
-            for j in range(n):
-                c = c0 + j
-                mx(
-                    ps[:, P * j : P * (j + 1)],
-                    sxq[:, P * c : P * (c + 1)],
-                    sxs[:, P * c : P * (c + 1)],
-                    bsq[:, 0:NP],
-                    bss[:, 0:NP],
-                )
-            for j in range(n):
-                sl = slice(P * j, P * (j + 1))
-                mx(pa[:, sl], axq[:, sl], axc[:, sl], bsq[:, NP : 2 * NP], bss[:, NP : 2 * NP])
-            for j in range(n):
-                sl = slice(P * j, P * (j + 1))
-                mx(pc[:, sl], axq[:, sl], axc[:, sl], bsq[:, 0:NP], bss[:, 0:NP])
-            unit[("ps", c0)] = ps
-            unit[("pa", c0)] = pa
-            unit[("pc", c0)] = pc
+        def c_pass(g):
+            pc = bank(PC_BANK, [P, 512], F32, "pc%d" % g)
+            for j in range(4):
+                mx(pc[:, cols(j)], axq[:, cols(4 * g + j)], axc[:, cols(4 * g + j)], bpq[:], bpc[:])
+            unit[("pc", g)] = pc
 
-        def fin_s(c0, n):
-            w = P * n
-            acc = fin_pool.tile([P, 512], F32, name="acc%d" % c0, tag="acc")
-            unit[("acc", c0)] = acc
+        def a_pass(g):
+            pa = bank(PA_BANK, [P, 512], F32, "pa%d" % g)
+            for j in range(4):
+                mx(pa[:, cols(j)], axq[:, cols(4 * g + j)], axc[:, cols(4 * g + j)], spq[:], spc[:])
+            unit[("pa", g)] = pa
+
+        def s_pass(g):
+            ps = bank(PS_BANKS[g % 2], [P, 512], F32, "ps%d" % g)
+            for j in range(4):
+                mx(ps[:, cols(j)], unit[("sxq", g)][:, cols(j)], unit[("sxc", g)][:, cols(j)], bpq[:], bpc[:])
+            unit[("ps", g)] = ps
+
+        def add_in(g, product, gain, first=False):
+            if first:
+                unit[("acc", g)] = fin_pool.tile([P, 512], F32, name="acc%d" % g, tag="acc", bufs=5)
+            acc = unit[("acc", g)]
             nc.vector.scalar_tensor_tensor(
-                out=acc[:, 0:w],
-                in0=unit[("ps", c0)][:, 0:w],
-                scalar=b32[:, 0:1],
-                in1=unit[("kb", c0)][:, 0:w],
+                out=acc[:],
+                in0=unit[(product, g)][:],
+                scalar=gain[:, 0:1],
+                in1=unit[("kb", g)][:] if first else acc[:],
                 op0=ALU.mult,
                 op1=ALU.add,
             )
 
-        def fin_a(c0, n):
-            w = P * n
-            acc = unit[("acc", c0)]
-            nc.vector.scalar_tensor_tensor(
-                out=acc[:, 0:w], in0=unit[("pa", c0)][:, 0:w], scalar=a32[:, 0:1], in1=acc[:, 0:w], op0=ALU.mult, op1=ALU.add
-            )
+        def store(g):
+            nc.sync.dma_start(out=out_rows[:, cols(g, 512)], in_=unit[("acc", g)][:])
 
-        def fin_c(c0, n):
-            w = P * n
-            acc = unit[("acc", c0)]
-            nc.vector.scalar_tensor_tensor(
-                out=acc[:, 0:w], in0=unit[("pc", c0)][:, 0:w], scalar=t32[:, 0:1], in1=acc[:, 0:w], op0=ALU.mult, op1=ALU.add
-            )
-            nc.sync.dma_start(out=out_rows[:, P * c0 : P * c0 + w], in_=acc[:, 0:w])
-
-        def fin(c0, n):
-            fin_s(c0, n)
-            fin_a(c0, n)
-            fin_c(c0, n)
-
-        o2_pass(0)
-        o2_pass(1)
-        q_s(NG - 1)
-        nc.vector.tensor_tensor(out=bp32[:], in0=pf[:], in1=sp32[:], op=ALU.mult)
-        nc.vector.tensor_copy(
-            out=gbs[:, 0:512].rearrange("p (m t) -> p m t", t=4), in_=bp32[:].rearrange("p (t m) -> p m t", t=4)
+        t_a(2 * NG - 1)
+        o1_pass(0)
+        pf2 = bank(PS_BANKS[0], [P, 512], F32, "pf2")
+        for t in range(4):
+            mx(pf2[:, cols(t)], fq1[:, cols(t)], fs1[:, cols(t)], pq[:], pscl[:])
+        nc.scalar.activation(
+            out=gsp[:].rearrange("p (m t) -> p m t", t=4), in_=pf2[:].rearrange("p (t m) -> p m t", t=4), func=ACT.Sigmoid
         )
-        nc.vector.tensor_copy(
-            out=gbs[:, 512:1024].rearrange("p (m t) -> p m t", t=4), in_=sp32[:].rearrange("p (t m) -> p m t", t=4)
-        )
-        quantise(bsq[:], bss[:], gbs[:])
-        kr = bank(5, [P, NP], F32, "kr")
+        e_a(2 * NG - 2, nc.vector.tensor_copy)
+        q_a(NG - 2)
+        e_a(2 * NG - 1, nc.vector.tensor_copy)
+        k_b(0)
+        for c in range(1, 4):
+            o1_pass(c)
+        c_pass(0)
+        quantise(spq[:], spc[:], gsp[:])
+        q_a(NG - 1)
 
-        for y in range(NG):
-            last = y == NG - 1
-            if y >= 1:
-                t_a(4 * y - 2, 2, AT_ODD)
-            silu(4 * y)
-            silu(4 * y + 1)
-            o2_pass(4 * y + 2)
-            o2_pass(4 * y + 3)
-            if y >= 2:
-                k_b(4 * (y - 2), 4)
-                s_2(4 * (y - 2), 4)
-            if y >= 1:
-                e_a(4 * y - 2, 2, ea_engine(2 * y - 1))
-            t_a(4 * y, 2, AT_EVEN)
-            if y >= 2:
-                fin_s(4 * (y - 2), 4)
-            if y >= 1:
-                q_a(4 * (y - 1), 4)
-            if y >= 2:
-                fin_a(4 * (y - 2), 4)
-            silu(4 * y + 2)
-            silu(4 * y + 3)
-            if not last:
-                o2_pass(4 * y + 4)
-                o2_pass(4 * y + 5)
-            if y == 0:
-                for t in range(4):
-                    nc.tensor.matmul(
-                        kr[:], lhsT=ones_f[:], rhs=bp32[:, P * t : P * (t + 1)], start=(t == 0), stop=(t == 3)
-                    )
-            e_a(4 * y, 2, nc.scalar.copy if last else ea_engine(2 * y))
-            if y >= 2:
-                fin_c(4 * (y - 2), 4)
-            if y == 0:
-                nc.vector.tensor_scalar_mul(out=krow[:], in0=kr[:], scalar1=nb32[:, 0:1])
-
-        c0 = NCH - 4
-        t_a(c0 + 2, 1, 1)
-        t_a(c0 + 3, 1, 2)
-        k_b(c0 - 4, 4)
-        s_2(c0 - 4, 4)
-        e_a(c0 + 2, 1, nc.scalar.copy)
-        e_a(c0 + 3, 1, nc.scalar.copy)
-        fin_s(c0 - 4, 4)
-        q_a(c0, 2)
-        fin_a(c0 - 4, 4)
-        k_b(c0, 2)
-        s_2(c0, 2, (0, 3, 4))
-        q_a(c0 + 2, 2)
-        fin_c(c0 - 4, 4)
-        k_b(c0 + 2, 2)
-        s_2(c0 + 2, 2)
-        fin_s(c0, 2)
-        fin_s(c0 + 2, 2)
-        fin_a(c0, 2)
-        fin_a(c0 + 2, 2)
-        fin_c(c0, 2)
-        fin_c(c0 + 2, 2)
+        for i in range(NG + 2):
+            for c4 in range(4):
+                if i < NG:
+                    sigmoid(4 * i + c4)
+                if i + 1 < NG:
+                    o1_pass(4 * (i + 1) + c4)
+                if c4 == 0:
+                    if 1 <= i <= NG:
+                        q_s(i - 1)
+                    if i + 1 < NG:
+                        k_b(i + 1)
+                if c4 == 1:
+                    if 1 <= i <= NG:
+                        add_in(i - 1, "pa", a32)
+                    if i < NG:
+                        a_pass(i)
+                if c4 == 2:
+                    if i < NG:
+                        add_in(i, "pc", t32, first=True)
+                    if i + 1 < NG:
+                        c_pass(i + 1)
+                if c4 == 3:
+                    if i >= 2:
+                        add_in(i - 2, "ps", b32)
+                        store(i - 2)
+                    if 1 <= i <= NG:
+                        s_pass(i - 1)

@@ -69,6 +69,7 @@ def tile_tverskylayer_pa_t_kernel(tc, x, features, prototypes, alpha, beta, thet
         axq = const.tile([P, B], U32, name="axq", align_bytes=64)
         axc = const.tile([P, B], U8, name="axc", align_bytes=64)
         rs = const.tile([P, NCH], F32, name="rs")
+        rsa = const.tile([P, NCH], F32, name="rsa")
         bp32 = const.tile([P, F], F32, name="bp32")
         gbp = const.tile([P, 4 * NP], BF16, name="gbp", align_bytes=64)
         gsp = const.tile([P, 4 * NP], BF16, name="gsp", align_bytes=64)
@@ -185,8 +186,8 @@ def tile_tverskylayer_pa_t_kernel(tc, x, features, prototypes, alpha, beta, thet
         t_x(1, 0)
         t_x(1, 1)
         load_x(7)
-        e_x(0, 1, nc.vector.tensor_copy)
         q_x(0, 0, 2)
+        e_x(0, 1, nc.vector.tensor_copy)
         e_x(1, 0, nc.vector.tensor_copy)
         q_x(0, 2, 2)
         e_x(1, 1, nc.vector.tensor_copy)
@@ -289,17 +290,12 @@ def tile_tverskylayer_pa_t_kernel(tc, x, features, prototypes, alpha, beta, thet
             unit[("sxc", g)] = sxc
 
         def k_b(g):
-            rsa = fin_pool.tile([P, 4], F32, name="rsa%d" % g, tag="rsa")
-            nc.gpsimd.tensor_scalar(
-                out=rsa[:], in0=rs[:, cols(g, 4)], scalar1=na32[:, 0:1], scalar2=0.0, op0=ALU.mult, op1=ALU.add
-            )
             kb = fin_pool.tile([P, 512], F32, name="kb%d" % g, tag="kb")
-            nc.gpsimd.tensor_tensor(
-                out=kb[:].rearrange("p (c q) -> p c q", c=4),
-                in0=krow[:].unsqueeze(1).to_broadcast([P, 4, NP]),
-                in1=rsa[:].unsqueeze(2).to_broadcast([P, 4, NP]),
-                op=ALU.add,
-            )
+            for j in range(4):
+                c = 4 * g + j
+                nc.gpsimd.tensor_scalar(
+                    out=kb[:, cols(j)], in0=krow[:], scalar1=1.0, scalar2=rsa[:, c : c + 1], op0=ALU.mult, op1=ALU.add
+                )
             unit[("kb", g)] = kb
 
         def c_pass(g):
@@ -347,6 +343,7 @@ def tile_tverskylayer_pa_t_kernel(tc, x, features, prototypes, alpha, beta, thet
         e_a(2 * NG - 2, nc.vector.tensor_copy)
         q_a(NG - 2)
         e_a(2 * NG - 1, nc.vector.tensor_copy)
+        nc.gpsimd.tensor_scalar(out=rsa[:], in0=rs[:], scalar1=na32[:, 0:1], scalar2=0.0, op0=ALU.mult, op1=ALU.add)
         k_b(0)
         for c in range(1, 4):
             o1_pass(c)

from contextlib import ExitStack

import concourse.mybir as mybir
from concourse.masks import make_identity

F32 = mybir.dt.float32
BF16 = mybir.dt.bfloat16
U32 = mybir.dt.uint32
U8 = mybir.dt.uint8
FP8X4 = mybir.dt.float8_e4m3fn_x4
ACT = mybir.ActivationFunctionType
ALU = mybir.AluOpType

P = 128
B, D, F, NP = 8192, 512, 512, 128
NCH = B // P
NG = NCH // 4
FLOPS = 2 * (B + NP) * D * F + 3 * 2 * B * F * NP

XT_BANKS = (0, 1, 2)
O2_BANKS = (3, 4, 5)
AT_BANKS = (6, 7)
O1_BANKS = (0, 3, 4, 5)
PS_BANKS = (1, 2)
PA_BANK = 6
PC_BANK = 7


def tile_tverskylayer_pa_t_kernel(tc, x, features, prototypes, alpha, beta, theta, out):
    nc = tc.nc
    with ExitStack() as ctx:
        ctx.enter_context(tc.manual_schedule())
        const = ctx.enter_context(tc.tile_pool(name="const", bufs=1))
        xin_pool = ctx.enter_context(tc.tile_pool(name="xin", bufs=6))
        grp_pool = ctx.enter_context(tc.tile_pool(name="grp", bufs=3))
        ax_pool = ctx.enter_context(tc.tile_pool(name="axp", bufs=6))
        fin_pool = ctx.enter_context(tc.tile_pool(name="fin", bufs=3))
        psum = ctx.enter_context(tc.psum_pool(name="ps", bufs=1))

        def bank(i, shape, dtype, name):
            return psum.tile(shape, dtype, name=name, tag="bank%d" % i)

        x_rows = x.rearrange("(p c) d -> p (c d)", c=NCH)
        out_rows = out.rearrange("(p c) q -> p (c q)", c=NCH)

        ident_f = const.tile([P, P], F32, name="ident_f")
        make_identity(nc, ident_f[:])
        ones_f = const.tile([P, P], F32, name="ones_f")
        nc.vector.memset(ones_f[:], 1.0)
        warm = const.tile([P, 1], F32, name="warm")
        nc.scalar.activation(out=warm[:], in_=ones_f[:, 0:1], func=ACT.Silu)

        f_sb = const.tile([P, 4 * D], BF16, name="f_sb")
        p_sb = const.tile([P, D], BF16, name="p_sb")
        a_bf = const.tile([P, 1], BF16, name="a_bf")
        b_bf = const.tile([P, 1], BF16, name="b_bf")
        t_bf = const.tile([P, 1], BF16, name="t_bf")
        gf1 = const.tile([P, 4 * F], BF16, name="gf1", align_bytes=64)
        gf2 = const.tile([P, 4 * F], BF16, name="gf2", align_bytes=64)
        gp = const.tile([P, 4 * NP], BF16, name="gp", align_bytes=64)
        fq1 = const.tile([P, F], U32, name="fq1", align_bytes=64)
        fs1 = const.tile([P, F], U8, name="fs1", align_bytes=64)
        fq2 = const.tile([P, F], U32, name="fq2", align_bytes=64)
        fs2 = const.tile([P, F], U8, name="fs2", align_bytes=64)
        pq = const.tile([P, NP], U32, name="pq", align_bytes=64)
        pscl = const.tile([P, NP], U8, name="pscl", align_bytes=64)
        xq = const.tile([P, B], U32, name="xq", align_bytes=64)
        xs = const.tile([P, B], U8, name="xs", align_bytes=64)
        axq = const.tile([P, B], U32, name="axq", align_bytes=64)
        axc = const.tile([P, B], U8, name="axc", align_bytes=64)
        rs = const.tile([P, NCH], F32, name="rs")
        rsa = const.tile([P, NCH], F32, name="rsa")
        bp32 = const.tile([P, F], F32, name="bp32")
        gbp = const.tile([P, 4 * NP], BF16, name="gbp", align_bytes=64)
        gsp = const.tile([P, 4 * NP], BF16, name="gsp", align_bytes=64)
        bpq = const.tile([P, NP], U32, name="bpq", align_bytes=64)
        bpc = const.tile([P, NP], U8, name="bpc", align_bytes=64)
        spq = const.tile([P, NP], U32, name="spq", align_bytes=64)
        spc = const.tile([P, NP], U8, name="spc", align_bytes=64)
        krow = const.tile([P, NP], F32, name="krow")
        a32 = const.tile([P, 1], F32, name="a32")
        b32 = const.tile([P, 1], F32, name="b32")
        t32 = const.tile([P, 1], F32, name="t32")
        na32 = const.tile([P, 1], F32, name="na32")
        nb32 = const.tile([P, 1], F32, name="nb32")

        def word_transposes(src_words, first_chunk, n_chunks, pbank):
            for j in range(n_chunks):
                for u in range(2):
                    nc.tensor.transpose(
                        pbank[:, P * (2 * j + u) : P * (2 * j + u + 1)],
                        src_words[:, 256 * (first_chunk + j) + P * u : 256 * (first_chunk + j) + P * (u + 1)],
                        ident_f[:],
                    )

        def exit_words(copy, dst_words, first_chunk, n_chunks, pbank):
            copy(
                out=dst_words[:, 256 * first_chunk : 256 * (first_chunk + n_chunks)].rearrange(
                    "p (c b u) -> p c b u", c=n_chunks, u=2
                ),
                in_=pbank[:, 0 : 256 * n_chunks].rearrange("p (c u b) -> p c b u", c=n_chunks, u=2),
            )

        def quantise(codes, scales, src):
            nc.vector.quantize_mx(out=codes.bitcast(FP8X4), scales=scales, in_=src)

        def mx(o, l, ls, r, rs_):
            nc.tensor.matmul_mx(
                out=o, lhsT=l.bitcast(FP8X4), lhsT_scale=ls, rhs=r.bitcast(FP8X4), rhs_scale=rs_, start=True, stop=True
            )

        def cols(i, w=P):
            return slice(w * i, w * (i + 1))

        xin = {}
        xt = {}
        gx = {}

        def load_x(g, pieces=1):
            xin[g] = xin_pool.tile([P, 4 * D], BF16, name="xin%d" % g, tag="xin")
            w = 4 * D // pieces
            for k in range(pieces):
                nc.sync.dma_start(
                    out=xin[g][:, w * k : w * (k + 1)], in_=x_rows[:, 4 * D * g + w * k : 4 * D * g + w * (k + 1)]
                )

        def t_x(g, k):
            xt[(g, k)] = bank(XT_BANKS[(2 * g + k) % 3], [P, 512], F32, "xt%d_%d" % (g, k))
            word_transposes(xin[g][:].bitcast(F32), 2 * k, 2, xt[(g, k)])

        def e_x(g, k, copy):
            if k == 0:
                gx[g] = grp_pool.tile([P, 2048], BF16, name="gx%d" % g, tag="gx", align_bytes=64)
            exit_words(copy, gx[g][:].bitcast(F32), 2 * k, 2, xt[(g, k)])

        def q_x(g, first=0, n=4):
            lo, hi = 512 * g + P * first, 512 * g + P * (first + n)
            quantise(xq[:, lo:hi], xs[:, lo:hi], gx[g][:, 512 * first : 512 * (first + n)])

        o2 = {}
        axs = {}
        at = {}
        ga = {}

        def o2_pass(c):
            o2[c] = bank(O2_BANKS[c % 3], [P, 512], F32, "o2_%d" % c)
            mx(o2[c][:], xq[:, cols(c)], xs[:, cols(c)], fq2[:], fs2[:])

        def silu(c):
            axs[c] = ax_pool.tile([P, 512], BF16, name="axs%d" % c, tag="axs")
            nc.scalar.activation(out=axs[c][:], in_=o2[c][:], func=ACT.Silu, accum_out=rs[:, c : c + 1])

        def t_a(h):
            at[h] = bank(AT_BANKS[h % 2], [P, 512], F32, "at%d" % h)
            for j in range(2):
                word_transposes(axs[2 * h + j][:].bitcast(F32), 0, 1, at[h][:, 256 * j : 256 * (j + 1)])

        def e_a(h, copy):
            g, k = h // 2, h % 2
            if k == 0:
                ga[g] = grp_pool.tile([P, 2048], BF16, name="ga%d" % g, tag="ga", align_bytes=64)
            exit_words(copy, ga[g][:].bitcast(F32), 2 * k, 2, at[h])

        def q_a(g):
            quantise(axq[:, cols(g, 512)], axc[:, cols(g, 512)], ga[g][:])

        nc.sync.dma_start(out=f_sb[:], in_=features.rearrange("(p t) d -> p (t d)", t=4))
        load_x(0, pieces=2)
        for g in range(1, 6):
            load_x(g)
        gf1w = gf1[:].bitcast(F32)
        gf2w = gf2[:].bitcast(F32)
        ft = [bank(O2_BANKS[j], [P, 512], F32, "ft%d" % j) for j in range(2)]
        for j in range(2):
            word_transposes(f_sb[:].bitcast(F32), 2 * j, 2, ft[j])
        for j, copy in ((0, nc.vector.tensor_copy), (1, nc.scalar.copy)):
            copy(
                out=gf2w[:, cols(j, 512)].rearrange("p (m e u) -> p m e u", e=2, u=2),
                in_=ft[j][:].rearrange("p (e u m) -> p m e u", e=2, u=2),
            )
        t_x(0, 0)
        t_x(0, 1)
        load_x(6)
        quantise(fq2[:], fs2[:], gf2[:])
        e_x(0, 0, nc.scalar.copy)
        t_x(1, 0)
        t_x(1, 1)
        load_x(7)
        q_x(0, 0, 2)
        e_x(0, 1, nc.vector.tensor_copy)
        e_x(1, 0, nc.vector.tensor_copy)
        q_x(0, 2, 2)
        e_x(1, 1, nc.vector.tensor_copy)
        o2_pass(0)
        o2_pass(1)

        for y in range(NG):
            more_x = y + 2 < NG
            if y >= 1:
                t_a(2 * y - 1)
            if more_x:
                t_x(y + 2, 0)
            if y == NG - 2:
                pt = bank(XT_BANKS[0], [P, 512], F32, "pt")
                word_transposes(p_sb[:].bitcast(F32), 0, 1, pt)
            silu(4 * y)
            silu(4 * y + 1)
            o2_pass(4 * y + 2)
            o2_pass(4 * y + 3)
            if y >= 1:
                e_a(2 * y - 2, nc.vector.tensor_copy)
            if y + 1 < NG:
                q_x(y + 1)
            if y >= 1:
                e_a(2 * y - 1, nc.scalar.copy)
            if more_x:
                e_x(y + 2, 0, nc.vector.tensor_copy)
            t_a(2 * y)
            if more_x:
                t_x(y + 2, 1)
            if y + 8 < NG:
                load_x(y + 8)
            if y == 8:
                nc.sync.dma_start(out=p_sb[:], in_=prototypes)
                nc.sync.dma_start(out=a_bf[:], in_=alpha.partition_broadcast(P))
                nc.sync.dma_start(out=b_bf[:], in_=beta.partition_broadcast(P))
                nc.sync.dma_start(out=t_bf[:], in_=theta.partition_broadcast(P))
            if y >= 2:
                q_a(y - 2)
            if y == NG - 1:
                pf = bank(XT_BANKS[1], [P, 512], F32, "pf")
                for t in range(4):
                    mx(pf[:, cols(t)], fq1[:, cols(t)], fs1[:, cols(t)], pq[:], pscl[:])
                nc.scalar.activation(out=bp32[:], in_=pf[:], func=ACT.Silu)
            silu(4 * y + 2)
            silu(4 * y + 3)
            if y + 1 < NG:
                o2_pass(4 * y + 4)
                o2_pass(4 * y + 5)
            if more_x:
                e_x(y + 2, 1, nc.vector.tensor_copy)
            if y == NG - 2:
                exit_words(nc.vector.tensor_copy, gp[:].bitcast(F32), 0, 1, pt)
                for j in range(2):
                    nc.vector.tensor_copy(
                        out=gf1w[:, cols(j, 512)].rearrange("p (e m u) -> p e m u", e=2, u=2),
                        in_=gf2w[:, cols(j, 512)].rearrange("p (m e u) -> p e m u", e=2, u=2),
                    )
                quantise(pq[:], pscl[:], gp[:])
                quantise(fq1[:], fs1[:], gf1[:])
                nc.vector.tensor_copy(out=a32[:], in_=a_bf[:])
                nc.vector.tensor_copy(out=b32[:], in_=b_bf[:])
                nc.vector.tensor_copy(out=t32[:], in_=t_bf[:])
                nc.vector.tensor_scalar_mul(out=na32[:], in0=a32[:], scalar1=-1.0)
                nc.vector.tensor_scalar_mul(out=nb32[:], in0=b32[:], scalar1=-1.0)
            if y == NG - 1:
                kr = bank(XT_BANKS[2], [P, NP], F32, "kr")
                for t in range(4):
                    nc.tensor.matmul(kr[:], lhsT=ones_f[:], rhs=bp32[:, cols(t)], start=(t == 0), stop=(t == 3))
                nc.vector.tensor_copy(
                    out=gbp[:].rearrange("p (m t) -> p m t", t=4), in_=bp32[:].rearrange("p (t m) -> p m t", t=4)
                )
                nc.vector.tensor_scalar_mul(out=krow[:], in0=kr[:], scalar1=nb32[:, 0:1])
                quantise(bpq[:], bpc[:], gbp[:])

        o1 = {}
        gs = {}
        unit = {}

        def o1_pass(c):
            o1[c] = bank(O1_BANKS[c % 4], [P, 512], F32, "o1_%d" % c)
            for t in range(4):
                mx(o1[c][:, cols(t)], fq1[:, cols(t)], fs1[:, cols(t)], xq[:, cols(c)], xs[:, cols(c)])

        def sigmoid(c):
            g, c4 = c // 4, c % 4
            if c4 == 0:
                gs[g] = grp_pool.tile([P, 2048], BF16, name="gs%d" % g, tag="gs", align_bytes=64)
            nc.scalar.activation(
                out=gs[g][:, cols(c4, 512)].rearrange("p (b t) -> p b t", t=4),
                in_=o1[c][:].rearrange("p (t b) -> p b t", t=4),
                func=ACT.Sigmoid,
            )

        def q_s(g):
            sxq = fin_pool.tile([P, 512], U32, name="sxq%d" % g, tag="sxq", align_bytes=64)
            sxc = fin_pool.tile([P, 512], U8, name="sxc%d" % g, tag="sxc", align_bytes=64)
            quantise(sxq[:], sxc[:], gs[g][:])
            unit[("sxq", g)] = sxq
            unit[("sxc", g)] = sxc

        def k_b(g):
            kb = fin_pool.tile([P, 512], F32, name="kb%d" % g, tag="kb")
            for j in range(4):
                c = 4 * g + j
                nc.gpsimd.tensor_scalar(
                    out=kb[:, cols(j)], in0=krow[:], scalar1=1.0, scalar2=rsa[:, c : c + 1], op0=ALU.mult, op1=ALU.add
                )
            unit[("kb", g)] = kb

        def c_pass(g):
            pc = bank(PC_BANK, [P, 512], F32, "pc%d" % g)
            for j in range(4):
                mx(pc[:, cols(j)], axq[:, cols(4 * g + j)], axc[:, cols(4 * g + j)], bpq[:], bpc[:])
            unit[("pc", g)] = pc

        def a_pass(g):
            pa = bank(PA_BANK, [P, 512], F32, "pa%d" % g)
            for j in range(4):
                mx(pa[:, cols(j)], axq[:, cols(4 * g + j)], axc[:, cols(4 * g + j)], spq[:], spc[:])
            unit[("pa", g)] = pa

        def s_pass(g):
            ps = bank(PS_BANKS[g % 2], [P, 512], F32, "ps%d" % g)
            for j in range(4):
                mx(ps[:, cols(j)], unit[("sxq", g)][:, cols(j)], unit[("sxc", g)][:, cols(j)], bpq[:], bpc[:])
            unit[("ps", g)] = ps

        def add_in(g, product, gain, first=False):
            if first:
                unit[("acc", g)] = fin_pool.tile([P, 512], F32, name="acc%d" % g, tag="acc", bufs=5)
            acc = unit[("acc", g)]
            nc.vector.scalar_tensor_tensor(
                out=acc[:],
                in0=unit[(product, g)][:],
                scalar=gain[:, 0:1],
                in1=unit[("kb", g)][:] if first else acc[:],
                op0=ALU.mult,
                op1=ALU.add,
            )

        def store(g):
            nc.sync.dma_start(out=out_rows[:, cols(g, 512)], in_=unit[("acc", g)][:])

        t_a(2 * NG - 1)
        o1_pass(0)
        pf2 = bank(PS_BANKS[0], [P, 512], F32, "pf2")
        for t in range(4):
            mx(pf2[:, cols(t)], fq1[:, cols(t)], fs1[:, cols(t)], pq[:], pscl[:])
        nc.scalar.activation(
            out=gsp[:].rearrange("p (m t) -> p m t", t=4), in_=pf2[:].rearrange("p (t m) -> p m t", t=4), func=ACT.Sigmoid
        )
        e_a(2 * NG - 2, nc.vector.tensor_copy)
        q_a(NG - 2)
        e_a(2 * NG - 1, nc.vector.tensor_copy)
        nc.gpsimd.tensor_scalar(out=rsa[:], in0=rs[:], scalar1=na32[:, 0:1], scalar2=0.0, op0=ALU.mult, op1=ALU.add)
        k_b(0)
        for c in range(1, 4):
            o1_pass(c)
        c_pass(0)
        quantise(spq[:], spc[:], gsp[:])
        q_a(NG - 1)

        for i in range(NG + 2):
            for c4 in range(4):
                if i < NG:
                    sigmoid(4 * i + c4)
                if i + 1 < NG:
                    o1_pass(4 * (i + 1) + c4)
                if c4 == 0:
                    if 1 <= i <= NG:
                        q_s(i - 1)
                    if i + 1 < NG:
                        k_b(i + 1)
                if c4 == 1:
                    if 1 <= i <= NG:
                        add_in(i - 1, "pa", a32)
                    if i < NG:
                        a_pass(i)
                if c4 == 2:
                    if i < NG:
                        add_in(i, "pc", t32, first=True)
                    if i + 1 < NG:
                        c_pass(i + 1)
                if c4 == 3:
                    if i >= 2:
                        add_in(i - 2, "ps", b32)
                        store(i - 2)
                    if 1 <= i <= NG:
                        s_pass(i - 1)
